import numpy as np
import ml_dtypes


def mxq(x, axis, fmt="e4m3"):
    dtype, down = {"e4m3": (ml_dtypes.float8_e4m3fn, 7), "e5m2": (ml_dtypes.float8_e5m2, 14)}[fmt]
    v = np.moveaxis(np.asarray(x, np.float32).astype(ml_dtypes.bfloat16).astype(np.float64), axis, -1)
    blocks = v.reshape(v.shape[:-1] + (-1, 32))
    amax = np.abs(blocks).max(-1, keepdims=True)
    byte = np.maximum(np.where(amax > 0, np.frexp(amax)[1] - 1 + 127, 0) - down, 1)
    scale = np.exp2(byte - 127.0)
    codes = (blocks / scale).astype(np.float32).astype(dtype).astype(np.float64)
    return np.moveaxis((codes * scale).reshape(v.shape), -1, axis)


WIDE = False


def mx_kscale(k):
    if not WIDE:
        return np.ones(k)
    levels = np.array([10, -10, 5, -5, 0])
    if k % 512:
        return np.exp2(np.random.permutation(np.resize(levels, k // 32))).repeat(32)
    a = np.empty((k // 512, 16))
    for p in range(k // 512):
        a[p, :8] = np.random.permutation(np.resize(levels, 8))
        for g in range(8):
            far = levels[np.abs(levels - a[p, g]) >= 10]
            a[p, g + 8] = far[np.random.randint(len(far))]
    return np.exp2(a.ravel()).repeat(32)


BF16 = ml_dtypes.bfloat16


def bf(x):
    return np.asarray(x, np.float32).astype(BF16)


def f64(x):
    return np.asarray(x).astype(np.float64)


E, D, H, C = 64, 1024, 512, 128


def silu(v):
    return v / (1.0 + np.exp(-v))


def setup_inputs():
    s = mx_kscale(D)
    t = mx_kscale(H)
    return {
        "node_embed": bf(np.random.standard_normal((E, D)) * s),
        "x_edge_c": bf(np.random.standard_normal((E, H)) * t),
        "ori": bf(np.random.standard_normal((E, D)) * s),
        "W1": bf(np.random.standard_normal((D, H)) * 1.0 / np.sqrt(D) / s[:, None]),
        "b1": bf(np.random.standard_normal(H) * 0.3),
        "W2": bf(np.random.standard_normal((H, D)) * 1.5 / np.sqrt(H) / t[:, None]),
        "b2": bf(np.random.standard_normal(D) * 0.3),
        "edge_num": E,
    }


def reference(node_embed, x_edge_c, ori, W1, b1, W2, b2, edge_num):
    x = np.concatenate([f64(node_embed), f64(ori)], axis=0)
    h = silu((mxq(x, 1, "e4m3") @ mxq(f64(W1), 0, "e4m3")) + f64(b1))
    h = (h.reshape(2, edge_num, H) * f64(x_edge_c).reshape(1, edge_num, H)).reshape(-1, H)
    y = silu((mxq(h, 1, "e4m3") @ mxq(f64(W2), 0, "e4m3")) + f64(b2))
    y = y.reshape(2 * edge_num, -1, C)
    return y[:edge_num] + y[edge_num:]

@@ -1,0 +1,230 @@
+import concourse.mybir as mybir
+from concourse.masks import make_identity
+
+F32 = mybir.dt.float32
+BF16 = mybir.dt.bfloat16
+U32 = mybir.dt.uint32
+U8 = mybir.dt.uint8
+FP8X4 = mybir.dt.float8_e4m3fn_x4
+SILU = mybir.ActivationFunctionType.Silu
+MULT = mybir.AluOpType.mult
+
+P = 128
+PACK = 4
+K_PASS = P * PACK
+E, D, H = 64, 1024, 512
+ROWS = 2 * E
+PASSES_1 = D // K_PASS
+CHUNKS_1 = H // P
+CHUNKS_2 = D // P
+PAIRS = CHUNKS_2 // 2
+LAG = 2
+PIECE = 512
+RUN = 4
+VECTOR_COLS = 256
+
+FLOPS = 2 * ROWS * D * H + 2 * ROWS * H * D
+
+
+def regroup_permuted(nc, grouped, raw):
+    out = grouped.rearrange("p (t m) j -> p m j t", t=PACK)
+    in_ = raw.rearrange("p j (m t) -> p m j t", t=PACK)
+    cut = VECTOR_COLS // PACK
+    nc.vector.tensor_copy(out=out[:, 0:cut], in_=in_[:, 0:cut])
+    nc.scalar.copy(out=out[:, cut:P], in_=in_[:, cut:P])
+
+
+def regroup(nc, grouped, raw):
+    nc.vector.tensor_copy(
+        out=grouped[:, 0:VECTOR_COLS, :].rearrange("p (c i) j -> p c j i", i=RUN),
+        in_=raw[:, :, 0:VECTOR_COLS].rearrange("p j (c i) -> p c j i", i=RUN),
+    )
+    nc.scalar.copy(
+        out=grouped[:, VECTOR_COLS:PIECE, :].rearrange("p (c i) j -> p c j i", i=RUN),
+        in_=raw[:, :, VECTOR_COLS:PIECE].rearrange("p j (c i) -> p c j i", i=RUN),
+    )
+
+
+def quantise(nc, codes, scales, grouped):
+    nc.vector.quantize_mx(out=codes.bitcast(FP8X4), scales=scales, in_=grouped)
+
+
+def tile_node_interaction_s_kernel(
+    tc, node_embed, x_edge_c, ori, W1, b1, W2, b2, edge_num, out
+):
+    nc = tc.nc
+    assert edge_num == E
+
+    with tc.tile_pool(name="sbuf", bufs=1) as sbuf, tc.psum_pool(
+        name="psum", bufs=8
+    ) as psum, tc.manual_schedule():
+        x_sb = sbuf.tile([P, 2, K_PASS], BF16)
+        for half, x_half in enumerate((node_embed, ori)):
+            nc.sync.dma_start(
+                out=x_sb[:, half, :], in_=x_half.rearrange("e (g k) -> (e g) k", g=PASSES_1)
+            )
+        w1_raw = sbuf.tile([P, PASSES_1, PACK, H], BF16)
+        w1_rows = W1.rearrange("(g p j) c -> g p j c", g=PASSES_1, j=PACK)
+        for g in range(PASSES_1):
+            nc.sync.dma_start(out=w1_raw[:, g], in_=w1_rows[g])
+        w2_raw = sbuf.tile([P, PACK, D], BF16)
+        w2_rows = W2.rearrange("(p j) n -> p j n", j=PACK)
+        for first in range(0, D, PIECE):
+            nc.sync.dma_start(
+                out=w2_raw[:, :, first : first + PIECE], in_=w2_rows[:, :, first : first + PIECE]
+            )
+        gate_sb = sbuf.tile([P, H], BF16)
+        nc.vector.memset(gate_sb[E:P, :], 0.0)
+        nc.scalar.dma_start(out=gate_sb[0:E, :], in_=x_edge_c)
+        b1_t = sbuf.tile([P, CHUNKS_1], BF16)
+        nc.scalar.dma_start(out=b1_t[:], in_=b1.rearrange("(p t) -> p t", t=PACK))
+        bias_rows = sbuf.tile([P, P], BF16)
+        nc.vector.memset(bias_rows[:], 0.0)
+        nc.scalar.dma_start(out=bias_rows[0:CHUNKS_2, :], in_=b2.rearrange("(c p) -> c p", p=P))
+
+        ident_f32 = sbuf.tile([P, P], F32)
+        make_identity(nc, ident_f32[:])
+        ident_bf16 = sbuf.tile([P, P], BF16)
+        make_identity(nc, ident_bf16[:])
+        warm = sbuf.tile([P, 1], F32)
+        nc.vector.memset(warm[:], 0.0)
+        nc.scalar.activation(out=warm[:], in_=warm[:], func=SILU)
+
+        x_grouped = sbuf.tile([P, PASSES_1 * ROWS * PACK], BF16, align_bytes=64)
+        x_grouped_words = x_grouped[:].bitcast(F32).rearrange(
+            "p (g half e u) -> p half g e u", g=PASSES_1, half=2, u=2
+        )
+        x_words = x_sb[:].bitcast(F32).rearrange("q half (p u) -> q half u p", u=2)
+        for half, copy in enumerate((nc.scalar.copy, nc.vector.tensor_copy)):
+            xt_ps = psum.tile([P, 2, E, PASSES_1], F32, tag="bank")
+            for u in range(2):
+                nc.tensor.transpose(
+                    xt_ps[:, u].rearrange("p e g -> p (e g)"), x_words[:, half, u, :], ident_f32[:]
+                )
+            copy(out=x_grouped_words[:, half], in_=xt_ps[:].rearrange("p u e g -> p g e u"))
+        x_codes = sbuf.tile([P, PASSES_1, ROWS], U32, align_bytes=64)
+        x_scales = sbuf.tile([P, PASSES_1, ROWS], U8, align_bytes=64)
+
+        gate_ps = psum.tile([P, PACK, P], BF16, tag="bank")
+        gate_cols = gate_sb[:].rearrange("e (m t) -> e t m", t=PACK)
+        for t in range(PACK):
+            nc.tensor.transpose(gate_ps[:, t], gate_cols[:, t], ident_bf16[:])
+        bias_ps = psum.tile([P, P], BF16, tag="bank")
+        nc.tensor.transpose(bias_ps[:], bias_rows[:], ident_bf16[:])
+
+        w1_grouped = sbuf.tile([P, PASSES_1, H, PACK], BF16, align_bytes=64)
+        w1_codes = sbuf.tile([P, PASSES_1, H], U32, align_bytes=64)
+        w1_scales = sbuf.tile([P, PASSES_1, H], U8, align_bytes=64)
+        a_ps = [psum.tile([P, ROWS], F32, tag="bank", name="a_ps%d" % c) for c in range(CHUNKS_1)]
+        regroup_permuted(nc, w1_grouped[:, 0], w1_raw[:, 0])
+        quantise(
+            nc,
+            x_codes[:].rearrange("p g r -> p (g r)"),
+            x_scales[:].rearrange("p g r -> p (g r)"),
+            x_grouped[:],
+        )
+        regroup_permuted(nc, w1_grouped[:, 1], w1_raw[:, 1])
+        for g in range(PASSES_1):
+            quantise(
+                nc, w1_codes[:, g], w1_scales[:, g], w1_grouped[:, g].rearrange("p w j -> p (w j)")
+            )
+            for c in range(CHUNKS_1):
+                nc.tensor.matmul_mx(
+                    out=a_ps[c][:],
+                    lhsT=w1_codes[:, g, c * P : (c + 1) * P].bitcast(FP8X4),
+                    lhsT_scale=w1_scales[:, g, c * P : (c + 1) * P],
+                    rhs=x_codes[:, g, :].bitcast(FP8X4),
+                    rhs_scale=x_scales[:, g, :],
+                    start=(g == 0),
+                    stop=(g == PASSES_1 - 1),
+                )
+
+        w2_grouped = sbuf.tile([P, D, PACK], BF16, align_bytes=64)
+        w2_codes = sbuf.tile([P, D], U32, align_bytes=64)
+        w2_scales = sbuf.tile([P, D], U8, align_bytes=64)
+
+        def regroup_w2(first):
+            regroup(
+                nc, w2_grouped[:, first : first + PIECE, :], w2_raw[:, :, first : first + PIECE]
+            )
+
+        def quantise_w2(first):
+            quantise(
+                nc,
+                w2_codes[:, first : first + PIECE],
+                w2_scales[:, first : first + PIECE],
+                w2_grouped[:, first : first + PIECE, :].rearrange("p w j -> p (w j)"),
+            )
+
+        regroup_w2(0)
+        bias_t = sbuf.tile([P, CHUNKS_2], F32)
+        nc.scalar.copy(out=bias_t[:], in_=bias_ps[:, 0:CHUNKS_2])
+        a_t = sbuf.tile([P, CHUNKS_1, ROWS], F32)
+        for c in range(CHUNKS_1):
+            nc.scalar.activation(
+                out=a_t[:, c, :], in_=a_ps[c][:], func=SILU, bias=b1_t[:, c : c + 1], scale=1.0
+            )
+        regroup_w2(PIECE)
+        quantise_w2(0)
+        h_grouped = sbuf.tile([P, 2, E * PACK], BF16, align_bytes=64)
+        for half in range(2):
+            nc.vector.tensor_tensor(
+                out=h_grouped[:, half, :].rearrange("p (e t) -> p e t", t=PACK),
+                in0=a_t[:, :, half * E : (half + 1) * E].rearrange("p t e -> p e t"),
+                in1=gate_ps[:, :, 0:E].rearrange("p t e -> p e t"),
+                op=MULT,
+            )
+        h_codes = sbuf.tile([P, ROWS], U32, align_bytes=64)
+        h_scales = sbuf.tile([P, ROWS], U8, align_bytes=64)
+        quantise(nc, h_codes[:], h_scales[:], h_grouped[:].rearrange("p half f -> p (half f)"))
+        quantise_w2(PIECE)
+
+        y_t = sbuf.tile([P, 2, CHUNKS_2, E], F32)
+
+        def layer_2_chunk(c):
+            y_ps = psum.tile([P, ROWS], F32, tag="bank")
+            nc.tensor.matmul_mx(
+                out=y_ps[:],
+                lhsT=w2_codes[:, c * P : (c + 1) * P].bitcast(FP8X4),
+                lhsT_scale=w2_scales[:, c * P : (c + 1) * P],
+                rhs=h_codes[:].bitcast(FP8X4),
+                rhs_scale=h_scales[:],
+                start=True,
+                stop=True,
+            )
+            nc.scalar.activation(
+                out=y_t[:, :, c, :],
+                in_=y_ps[:].rearrange("p (half e) -> p half e", half=2),
+                func=SILU,
+                bias=bias_t[:, c : c + 1],
+                scale=1.0,
+            )
+
+        out_sb = sbuf.tile([P, PAIRS, P], F32)
+        out_rows = out.rearrange("e (pair i) d -> i e pair d", i=2)
+
+        def close_pair(pair):
+            out_ps = psum.tile([P, P], F32, tag="bank")
+            for half in range(2):
+                nc.tensor.matmul(
+                    out=out_ps[:],
+                    lhsT=y_t[:, half, 2 * pair : 2 * pair + 2, :].rearrange("p c e -> p (c e)"),
+                    rhs=ident_f32[:],
+                    start=(half == 0),
+                    stop=(half == 1),
+                    is_transpose=True,
+                )
+            nc.vector.tensor_copy(out=out_sb[:, pair, :], in_=out_ps[:])
+            if pair % 2 == 1:
+                done = slice(pair - 1, pair + 1)
+                for i in range(2):
+                    nc.sync.dma_start(
+                        out=out_rows[i][:, done, :], in_=out_sb[i * E : (i + 1) * E, done, :]
+                    )
+
+        for step in range(PAIRS + LAG):
+            if step < PAIRS:
+                layer_2_chunk(2 * step)
+                layer_2_chunk(2 * step + 1)
+            if step >= LAG:
+                close_pair(step - LAG)

@@ -58,21 +58,6 @@ def tile_node_interaction_s_kernel(
     with tc.tile_pool(name="sbuf", bufs=1) as sbuf, tc.psum_pool(
         name="psum", bufs=8
     ) as psum, tc.manual_schedule():
-        x_sb = sbuf.tile([P, 2, K_PASS], BF16)
-        for half, x_half in enumerate((node_embed, ori)):
-            nc.sync.dma_start(
-                out=x_sb[:, half, :], in_=x_half.rearrange("e (g k) -> (e g) k", g=PASSES_1)
-            )
-        w1_raw = sbuf.tile([P, PASSES_1, PACK, H], BF16)
-        w1_rows = W1.rearrange("(g p j) c -> g p j c", g=PASSES_1, j=PACK)
-        for g in range(PASSES_1):
-            nc.sync.dma_start(out=w1_raw[:, g], in_=w1_rows[g])
-        w2_raw = sbuf.tile([P, PACK, D], BF16)
-        w2_rows = W2.rearrange("(p j) n -> p j n", j=PACK)
-        for first in range(0, D, PIECE):
-            nc.sync.dma_start(
-                out=w2_raw[:, :, first : first + PIECE], in_=w2_rows[:, :, first : first + PIECE]
-            )
         gate_sb = sbuf.tile([P, H], BF16)
         nc.vector.memset(gate_sb[E:P, :], 0.0)
         nc.scalar.dma_start(out=gate_sb[0:E, :], in_=x_edge_c)
@@ -81,6 +66,21 @@ def tile_node_interaction_s_kernel(
         bias_rows = sbuf.tile([P, P], BF16)
         nc.vector.memset(bias_rows[:], 0.0)
         nc.scalar.dma_start(out=bias_rows[0:CHUNKS_2, :], in_=b2.rearrange("(c p) -> c p", p=P))
+        w1_raw = sbuf.tile([P, PASSES_1, PACK, H], BF16)
+        w1_rows = W1.rearrange("(g p j) c -> g p j c", g=PASSES_1, j=PACK)
+        nc.sync.dma_start(out=w1_raw[:, 0], in_=w1_rows[0])
+        x_sb = sbuf.tile([P, 2, K_PASS], BF16)
+        for half, x_half in enumerate((node_embed, ori)):
+            nc.sync.dma_start(
+                out=x_sb[:, half, :], in_=x_half.rearrange("e (g k) -> (e g) k", g=PASSES_1)
+            )
+        nc.sync.dma_start(out=w1_raw[:, 1], in_=w1_rows[1])
+        w2_raw = sbuf.tile([P, PACK, D], BF16)
+        w2_rows = W2.rearrange("(p j) n -> p j n", j=PACK)
+        for first in range(0, D, PIECE):
+            nc.sync.dma_start(
+                out=w2_raw[:, :, first : first + PIECE], in_=w2_rows[:, :, first : first + PIECE]
+            )
 
         ident_f32 = sbuf.tile([P, P], F32)
         make_identity(nc, ident_f32[:])
@@ -89,6 +89,18 @@ def tile_node_interaction_s_kernel(
         warm = sbuf.tile([P, 1], F32)
         nc.vector.memset(warm[:], 0.0)
         nc.scalar.activation(out=warm[:], in_=warm[:], func=SILU)
+
+        w1_grouped = sbuf.tile([P, PASSES_1, H, PACK], BF16, align_bytes=64)
+        w1_codes = sbuf.tile([P, PASSES_1, H], U32, align_bytes=64)
+        w1_scales = sbuf.tile([P, PASSES_1, H], U8, align_bytes=64)
+
+        def quantise_w1(g):
+            quantise(
+                nc, w1_codes[:, g], w1_scales[:, g], w1_grouped[:, g].rearrange("p w j -> p (w j)")
+            )
+
+        regroup_permuted(nc, w1_grouped[:, 0], w1_raw[:, 0])
+        quantise_w1(0)
 
         x_grouped = sbuf.tile([P, PASSES_1 * ROWS * PACK], BF16, align_bytes=64)
         x_grouped_words = x_grouped[:].bitcast(F32).rearrange(
@@ -112,22 +124,16 @@ def tile_node_interaction_s_kernel(
         bias_ps = psum.tile([P, P], BF16, tag="bank")
         nc.tensor.transpose(bias_ps[:], bias_rows[:], ident_bf16[:])
 
-        w1_grouped = sbuf.tile([P, PASSES_1, H, PACK], BF16, align_bytes=64)
-        w1_codes = sbuf.tile([P, PASSES_1, H], U32, align_bytes=64)
-        w1_scales = sbuf.tile([P, PASSES_1, H], U8, align_bytes=64)
         a_ps = [psum.tile([P, ROWS], F32, tag="bank", name="a_ps%d" % c) for c in range(CHUNKS_1)]
-        regroup_permuted(nc, w1_grouped[:, 0], w1_raw[:, 0])
+        regroup_permuted(nc, w1_grouped[:, 1], w1_raw[:, 1])
         quantise(
             nc,
             x_codes[:].rearrange("p g r -> p (g r)"),
             x_scales[:].rearrange("p g r -> p (g r)"),
             x_grouped[:],
         )
-        regroup_permuted(nc, w1_grouped[:, 1], w1_raw[:, 1])
+        quantise_w1(1)
         for g in range(PASSES_1):
-            quantise(
-                nc, w1_codes[:, g], w1_scales[:, g], w1_grouped[:, g].rearrange("p w j -> p (w j)")
-            )
             for c in range(CHUNKS_1):
                 nc.tensor.matmul_mx(
                     out=a_ps[c][:],

@@ -18,30 +18,28 @@ PASSES_1 = D // K_PASS
 CHUNKS_1 = H // P
 CHUNKS_2 = D // P
 PAIRS = CHUNKS_2 // 2
-LAG = 2
 PIECE = 512
+PIECES_2 = D // PIECE
+CHUNKS_PIECE = PIECE // P
 RUN = 4
-VECTOR_COLS = 256
+VECTOR_W1 = (320, 320)
+VECTOR_W2 = (256, 224)
 
 FLOPS = 2 * ROWS * D * H + 2 * ROWS * H * D
 
 
-def regroup_permuted(nc, grouped, raw):
-    out = grouped.rearrange("p (t m) j -> p m j t", t=PACK)
-    in_ = raw.rearrange("p j (m t) -> p m j t", t=PACK)
-    cut = VECTOR_COLS // PACK
-    nc.vector.tensor_copy(out=out[:, 0:cut], in_=in_[:, 0:cut])
-    nc.scalar.copy(out=out[:, cut:P], in_=in_[:, cut:P])
-
-
-def regroup(nc, grouped, raw):
-    nc.vector.tensor_copy(
-        out=grouped[:, 0:VECTOR_COLS, :].rearrange("p (c i) j -> p c j i", i=RUN),
-        in_=raw[:, :, 0:VECTOR_COLS].rearrange("p j (c i) -> p c j i", i=RUN),
+def regroup_permuted(copy, grouped, raw, first, last):
+    m = slice(first // PACK, last // PACK)
+    copy(
+        out=grouped.rearrange("p (t m) j -> p m j t", t=PACK)[:, m],
+        in_=raw.rearrange("p j (m t) -> p m j t", t=PACK)[:, m],
     )
-    nc.scalar.copy(
-        out=grouped[:, VECTOR_COLS:PIECE, :].rearrange("p (c i) j -> p c j i", i=RUN),
-        in_=raw[:, :, VECTOR_COLS:PIECE].rearrange("p j (c i) -> p c j i", i=RUN),
+
+
+def regroup(copy, grouped, raw, first, last):
+    copy(
+        out=grouped[:, first:last, :].rearrange("p (c i) j -> p c j i", i=RUN),
+        in_=raw[:, :, first:last].rearrange("p j (c i) -> p c j i", i=RUN),
     )
 
 
@@ -75,12 +73,12 @@ def tile_node_interaction_s_kernel(
                 out=x_sb[:, half, :], in_=x_half.rearrange("e (g k) -> (e g) k", g=PASSES_1)
             )
         nc.sync.dma_start(out=w1_raw[:, 1], in_=w1_rows[1])
-        w2_raw = sbuf.tile([P, PACK, D], BF16)
         w2_rows = W2.rearrange("(p j) n -> p j n", j=PACK)
-        for first in range(0, D, PIECE):
-            nc.sync.dma_start(
-                out=w2_raw[:, :, first : first + PIECE], in_=w2_rows[:, :, first : first + PIECE]
-            )
+        w2_raw = []
+        for i in range(PIECES_2):
+            raw = sbuf.tile([P, PACK, PIECE], BF16, name="w2_raw%d" % i)
+            nc.sync.dma_start(out=raw[:], in_=w2_rows[:, :, i * PIECE : (i + 1) * PIECE])
+            w2_raw.append(raw)
 
         ident_f32 = sbuf.tile([P, P], F32)
         make_identity(nc, ident_f32[:])
@@ -99,7 +97,12 @@ def tile_node_interaction_s_kernel(
                 nc, w1_codes[:, g], w1_scales[:, g], w1_grouped[:, g].rearrange("p w j -> p (w j)")
             )
 
-        regroup_permuted(nc, w1_grouped[:, 0], w1_raw[:, 0])
+        def regroup_w1(g):
+            cut = VECTOR_W1[g]
+            regroup_permuted(nc.vector.tensor_copy, w1_grouped[:, g], w1_raw[:, g], 0, cut)
+            regroup_permuted(nc.scalar.copy, w1_grouped[:, g], w1_raw[:, g], cut, H)
+
+        regroup_w1(0)
         quantise_w1(0)
 
         x_grouped = sbuf.tile([P, PASSES_1 * ROWS * PACK], BF16, align_bytes=64)
@@ -107,13 +110,15 @@ def tile_node_interaction_s_kernel(
             "p (g half e u) -> p half g e u", g=PASSES_1, half=2, u=2
         )
         x_words = x_sb[:].bitcast(F32).rearrange("q half (p u) -> q half u p", u=2)
-        for half, copy in enumerate((nc.scalar.copy, nc.vector.tensor_copy)):
+        for half in range(2):
             xt_ps = psum.tile([P, 2, E, PASSES_1], F32, tag="bank")
             for u in range(2):
                 nc.tensor.transpose(
                     xt_ps[:, u].rearrange("p e g -> p (e g)"), x_words[:, half, u, :], ident_f32[:]
                 )
-            copy(out=x_grouped_words[:, half], in_=xt_ps[:].rearrange("p u e g -> p g e u"))
+            nc.scalar.copy(
+                out=x_grouped_words[:, half], in_=xt_ps[:].rearrange("p u e g -> p g e u")
+            )
         x_codes = sbuf.tile([P, PASSES_1, ROWS], U32, align_bytes=64)
         x_scales = sbuf.tile([P, PASSES_1, ROWS], U8, align_bytes=64)
 
@@ -125,7 +130,7 @@ def tile_node_interaction_s_kernel(
         nc.tensor.transpose(bias_ps[:], bias_rows[:], ident_bf16[:])
 
         a_ps = [psum.tile([P, ROWS], F32, tag="bank", name="a_ps%d" % c) for c in range(CHUNKS_1)]
-        regroup_permuted(nc, w1_grouped[:, 1], w1_raw[:, 1])
+        regroup_w1(1)
         quantise(
             nc,
             x_codes[:].rearrange("p g r -> p (g r)"),
@@ -145,24 +150,28 @@ def tile_node_interaction_s_kernel(
                     stop=(g == PASSES_1 - 1),
                 )
 
-        w2_grouped = sbuf.tile([P, D, PACK], BF16, align_bytes=64)
-        w2_codes = sbuf.tile([P, D], U32, align_bytes=64)
-        w2_scales = sbuf.tile([P, D], U8, align_bytes=64)
+        w2_grouped = []
+        w2_codes = []
+        w2_scales = []
+        for i in range(PIECES_2):
+            grouped = sbuf.tile([P, PIECE, PACK], BF16, align_bytes=64, name="w2_grouped%d" % i)
+            codes = sbuf.tile([P, PIECE], U32, align_bytes=64, name="w2_codes%d" % i)
+            scales = sbuf.tile([P, PIECE], U8, align_bytes=64, name="w2_scales%d" % i)
+            w2_grouped.append(grouped)
+            w2_codes.append(codes)
+            w2_scales.append(scales)
 
-        def regroup_w2(first):
-            regroup(
-                nc, w2_grouped[:, first : first + PIECE, :], w2_raw[:, :, first : first + PIECE]
-            )
+        def regroup_w2(copy, i, first, last):
+            regroup(copy, w2_grouped[i][:], w2_raw[i][:], first, last)
 
-        def quantise_w2(first):
+        def quantise_w2(i):
             quantise(
-                nc,
-                w2_codes[:, first : first + PIECE],
-                w2_scales[:, first : first + PIECE],
-                w2_grouped[:, first : first + PIECE, :].rearrange("p w j -> p (w j)"),
+                nc, w2_codes[i][:], w2_scales[i][:], w2_grouped[i][:].rearrange("p w j -> p (w j)")
             )
 
-        regroup_w2(0)
+        vector_half = VECTOR_W2[1] // 2
+        regroup_w2(nc.vector.tensor_copy, 0, 0, VECTOR_W2[0])
+        regroup_w2(nc.scalar.copy, 0, VECTOR_W2[0], PIECE)
         bias_t = sbuf.tile([P, CHUNKS_2], F32)
         nc.scalar.copy(out=bias_t[:], in_=bias_ps[:, 0:CHUNKS_2])
         a_t = sbuf.tile([P, CHUNKS_1, ROWS], F32)
@@ -170,7 +179,8 @@ def tile_node_interaction_s_kernel(
             nc.scalar.activation(
                 out=a_t[:, c, :], in_=a_ps[c][:], func=SILU, bias=b1_t[:, c : c + 1], scale=1.0
             )
-        regroup_w2(PIECE)
+        regroup_w2(nc.vector.tensor_copy, 1, 0, vector_half)
+        regroup_w2(nc.scalar.copy, 1, VECTOR_W2[1], PIECE)
         quantise_w2(0)
         h_grouped = sbuf.tile([P, 2, E * PACK], BF16, align_bytes=64)
         for half in range(2):
@@ -180,26 +190,32 @@ def tile_node_interaction_s_kernel(
                 in1=gate_ps[:, :, 0:E].rearrange("p t e -> p e t"),
                 op=MULT,
             )
+        regroup_w2(nc.vector.tensor_copy, 1, vector_half, VECTOR_W2[1])
         h_codes = sbuf.tile([P, ROWS], U32, align_bytes=64)
         h_scales = sbuf.tile([P, ROWS], U8, align_bytes=64)
         quantise(nc, h_codes[:], h_scales[:], h_grouped[:].rearrange("p half f -> p (half f)"))
-        quantise_w2(PIECE)
+        quantise_w2(1)
 
-        y_t = sbuf.tile([P, 2, CHUNKS_2, E], F32)
+        y_t = []
+        for pair in range(PAIRS):
+            y_pair = sbuf.tile([P, 2, 2, E], F32, name="y_t%d" % pair)
+            y_t.append(y_pair)
 
         def layer_2_chunk(c):
+            piece, place = divmod(c, CHUNKS_PIECE)
+            cols = slice(place * P, (place + 1) * P)
             y_ps = psum.tile([P, ROWS], F32, tag="bank")
             nc.tensor.matmul_mx(
                 out=y_ps[:],
-                lhsT=w2_codes[:, c * P : (c + 1) * P].bitcast(FP8X4),
-                lhsT_scale=w2_scales[:, c * P : (c + 1) * P],
+                lhsT=w2_codes[piece][:, cols].bitcast(FP8X4),
+                lhsT_scale=w2_scales[piece][:, cols],
                 rhs=h_codes[:].bitcast(FP8X4),
                 rhs_scale=h_scales[:],
                 start=True,
                 stop=True,
             )
             nc.scalar.activation(
-                out=y_t[:, :, c, :],
+                out=y_t[c // 2][:, :, c % 2, :],
                 in_=y_ps[:].rearrange("p (half e) -> p half e", half=2),
                 func=SILU,
                 bias=bias_t[:, c : c + 1],
@@ -214,7 +230,7 @@ def tile_node_interaction_s_kernel(
             for half in range(2):
                 nc.tensor.matmul(
                     out=out_ps[:],
-                    lhsT=y_t[:, half, 2 * pair : 2 * pair + 2, :].rearrange("p c e -> p (c e)"),
+                    lhsT=y_t[pair][:, half].rearrange("p i e -> p (i e)"),
                     rhs=ident_f32[:],
                     start=(half == 0),
                     stop=(half == 1),
@@ -228,9 +244,7 @@ def tile_node_interaction_s_kernel(
                         out=out_rows[i][:, done, :], in_=out_sb[i * E : (i + 1) * E, done, :]
                     )
 
-        for step in range(PAIRS + LAG):
-            if step < PAIRS:
-                layer_2_chunk(2 * step)
-                layer_2_chunk(2 * step + 1)
-            if step >= LAG:
-                close_pair(step - LAG)
+        for c in range(CHUNKS_2):
+            layer_2_chunk(c)
+        for pair in range(PAIRS):
+            close_pair(pair)

@@ -21,7 +21,7 @@ PAIRS = CHUNKS_2 // 2
 PIECE = 512
 PIECES_2 = D // PIECE
 CHUNKS_PIECE = PIECE // P
-RUN = 4
+RUN = 8
 VECTOR_W1 = (320, 320)
 VECTOR_W2 = (256, 224)
 
@@ -182,18 +182,18 @@ def tile_node_interaction_s_kernel(
         regroup_w2(nc.vector.tensor_copy, 1, 0, vector_half)
         regroup_w2(nc.scalar.copy, 1, VECTOR_W2[1], PIECE)
         quantise_w2(0)
-        h_grouped = sbuf.tile([P, 2, E * PACK], BF16, align_bytes=64)
-        for half in range(2):
-            nc.vector.tensor_tensor(
-                out=h_grouped[:, half, :].rearrange("p (e t) -> p e t", t=PACK),
-                in0=a_t[:, :, half * E : (half + 1) * E].rearrange("p t e -> p e t"),
-                in1=gate_ps[:, :, 0:E].rearrange("p t e -> p e t"),
-                op=MULT,
-            )
+        h_grouped = sbuf.tile([P, 2, E, PACK], BF16, align_bytes=64)
+        gate_rows = gate_ps[:, :, 0:E].rearrange("p t e -> p e t")
+        nc.vector.tensor_tensor(
+            out=h_grouped[:],
+            in0=a_t[:].rearrange("p t (half e) -> p half e t", half=2),
+            in1=gate_rows.unsqueeze(1).to_broadcast([P, 2, E, PACK]),
+            op=MULT,
+        )
         regroup_w2(nc.vector.tensor_copy, 1, vector_half, VECTOR_W2[1])
         h_codes = sbuf.tile([P, ROWS], U32, align_bytes=64)
         h_scales = sbuf.tile([P, ROWS], U8, align_bytes=64)
-        quantise(nc, h_codes[:], h_scales[:], h_grouped[:].rearrange("p half f -> p (half f)"))
+        quantise(nc, h_codes[:], h_scales[:], h_grouped[:].rearrange("p half e t -> p (half e t)"))
         quantise_w2(1)
 
         y_t = []

@@ -18,6 +18,7 @@ PASSES_1 = D // K_PASS
 CHUNKS_1 = H // P
 CHUNKS_2 = D // P
 PAIRS = CHUNKS_2 // 2
+IDLE_PASSES = 2
 PIECE = 512
 PIECES_2 = D // PIECE
 CHUNKS_PIECE = PIECE // P
@@ -54,8 +55,8 @@ def tile_node_interaction_s_kernel(
     assert edge_num == E
 
     with tc.tile_pool(name="sbuf", bufs=1) as sbuf, tc.psum_pool(
-        name="psum", bufs=8
-    ) as psum, tc.manual_schedule():
+        name="psum", bufs=7
+    ) as psum, tc.psum_pool(name="idle", bufs=1) as idle, tc.manual_schedule():
         gate_sb = sbuf.tile([P, H], BF16)
         nc.vector.memset(gate_sb[E:P, :], 0.0)
         nc.scalar.dma_start(out=gate_sb[0:E, :], in_=x_edge_c)
@@ -126,8 +127,22 @@ def tile_node_interaction_s_kernel(
         gate_cols = gate_sb[:].rearrange("e (m t) -> e t m", t=PACK)
         for t in range(PACK):
             nc.tensor.transpose(gate_ps[:, t], gate_cols[:, t], ident_bf16[:])
-        bias_ps = psum.tile([P, P], BF16, tag="bank")
-        nc.tensor.transpose(bias_ps[:], bias_rows[:], ident_bf16[:])
+
+        idle_ps = idle.tile([P, PIECE], F32)
+
+        def keep_busy(codes, scales):
+            for i in range(IDLE_PASSES):
+                nc.tensor.matmul_mx(
+                    out=idle_ps[:],
+                    lhsT=codes[:, 0:P].bitcast(FP8X4),
+                    lhsT_scale=scales[:, 0:P],
+                    rhs=codes.bitcast(FP8X4),
+                    rhs_scale=scales,
+                    start=True,
+                    stop=True,
+                )
+
+        keep_busy(w1_codes[:, 0], w1_scales[:, 0])
 
         a_ps = [psum.tile([P, ROWS], F32, tag="bank", name="a_ps%d" % c) for c in range(CHUNKS_1)]
         regroup_w1(1)
@@ -149,6 +164,9 @@ def tile_node_interaction_s_kernel(
                     start=(g == 0),
                     stop=(g == PASSES_1 - 1),
                 )
+
+        bias_ps = psum.tile([P, P], BF16, tag="bank")
+        nc.tensor.transpose(bias_ps[:], bias_rows[:], ident_bf16[:])
 
         w2_grouped = []
         w2_codes = []
@@ -172,16 +190,17 @@ def tile_node_interaction_s_kernel(
         vector_half = VECTOR_W2[1] // 2
         regroup_w2(nc.vector.tensor_copy, 0, 0, VECTOR_W2[0])
         regroup_w2(nc.scalar.copy, 0, VECTOR_W2[0], PIECE)
-        bias_t = sbuf.tile([P, CHUNKS_2], F32)
-        nc.scalar.copy(out=bias_t[:], in_=bias_ps[:, 0:CHUNKS_2])
         a_t = sbuf.tile([P, CHUNKS_1, ROWS], F32)
         for c in range(CHUNKS_1):
             nc.scalar.activation(
                 out=a_t[:, c, :], in_=a_ps[c][:], func=SILU, bias=b1_t[:, c : c + 1], scale=1.0
             )
+        bias_t = sbuf.tile([P, CHUNKS_2], F32)
+        nc.scalar.copy(out=bias_t[:], in_=bias_ps[:, 0:CHUNKS_2])
         regroup_w2(nc.vector.tensor_copy, 1, 0, vector_half)
         regroup_w2(nc.scalar.copy, 1, VECTOR_W2[1], PIECE)
         quantise_w2(0)
+        keep_busy(w2_codes[0][:], w2_scales[0][:])
         h_grouped = sbuf.tile([P, 2, E, PACK], BF16, align_bytes=64)
         gate_rows = gate_ps[:, :, 0:E].rearrange("p t e -> p e t")
         nc.vector.tensor_tensor(

@@ -130,19 +130,19 @@ def tile_node_interaction_s_kernel(
 
         idle_ps = idle.tile([P, PIECE], F32)
 
-        def keep_busy(codes, scales):
-            for i in range(IDLE_PASSES):
-                nc.tensor.matmul_mx(
-                    out=idle_ps[:],
-                    lhsT=codes[:, 0:P].bitcast(FP8X4),
-                    lhsT_scale=scales[:, 0:P],
-                    rhs=codes.bitcast(FP8X4),
-                    rhs_scale=scales,
-                    start=True,
-                    stop=True,
-                )
+        def idle_pass():
+            nc.tensor.matmul_mx(
+                out=idle_ps[:],
+                lhsT=w1_codes[:, 0, 0:P].bitcast(FP8X4),
+                lhsT_scale=w1_scales[:, 0, 0:P],
+                rhs=w1_codes[:, 0, :].bitcast(FP8X4),
+                rhs_scale=w1_scales[:, 0, :],
+                start=True,
+                stop=True,
+            )
 
-        keep_busy(w1_codes[:, 0], w1_scales[:, 0])
+        for i in range(IDLE_PASSES):
+            idle_pass()
 
         a_ps = [psum.tile([P, ROWS], F32, tag="bank", name="a_ps%d" % c) for c in range(CHUNKS_1)]
         regroup_w1(1)
@@ -187,7 +187,6 @@ def tile_node_interaction_s_kernel(
                 nc, w2_codes[i][:], w2_scales[i][:], w2_grouped[i][:].rearrange("p w j -> p (w j)")
             )
 
-        vector_half = VECTOR_W2[1] // 2
         regroup_w2(nc.vector.tensor_copy, 0, 0, VECTOR_W2[0])
         regroup_w2(nc.scalar.copy, 0, VECTOR_W2[0], PIECE)
         a_t = sbuf.tile([P, CHUNKS_1, ROWS], F32)
@@ -197,10 +196,16 @@ def tile_node_interaction_s_kernel(
             )
         bias_t = sbuf.tile([P, CHUNKS_2], F32)
         nc.scalar.copy(out=bias_t[:], in_=bias_ps[:, 0:CHUNKS_2])
-        regroup_w2(nc.vector.tensor_copy, 1, 0, vector_half)
+        regroup_w2(nc.vector.tensor_copy, 1, 0, VECTOR_W2[1])
         regroup_w2(nc.scalar.copy, 1, VECTOR_W2[1], PIECE)
-        quantise_w2(0)
-        keep_busy(w2_codes[0][:], w2_scales[0][:])
+        nc.tensor.matmul(
+            out=idle_ps[:],
+            lhsT=ident_bf16[:],
+            rhs=w2_grouped[1][:, 0:P, :].rearrange("p w j -> p (w j)"),
+            start=True,
+            stop=True,
+        )
+        idle_pass()
         h_grouped = sbuf.tile([P, 2, E, PACK], BF16, align_bytes=64)
         gate_rows = gate_ps[:, :, 0:E].rearrange("p t e -> p e t")
         nc.vector.tensor_tensor(
@@ -209,7 +214,7 @@ def tile_node_interaction_s_kernel(
             in1=gate_rows.unsqueeze(1).to_broadcast([P, 2, E, PACK]),
             op=MULT,
         )
-        regroup_w2(nc.vector.tensor_copy, 1, vector_half, VECTOR_W2[1])
+        quantise_w2(0)
         h_codes = sbuf.tile([P, ROWS], U32, align_bytes=64)
         h_scales = sbuf.tile([P, ROWS], U8, align_bytes=64)
         quantise(nc, h_codes[:], h_scales[:], h_grouped[:].rearrange("p half e t -> p (half e t)"))

@@ -18,8 +18,9 @@ PASSES_1 = D // K_PASS
 CHUNKS_1 = H // P
 CHUNKS_2 = D // P
 PAIRS = CHUNKS_2 // 2
-IDLE_PASSES = 2
 PIECE = 512
+HALF = PIECE // 2
+IDLE_PASSES = 4
 PIECES_2 = D // PIECE
 CHUNKS_PIECE = PIECE // P
 RUN = 8
@@ -128,21 +129,21 @@ def tile_node_interaction_s_kernel(
         for t in range(PACK):
             nc.tensor.transpose(gate_ps[:, t], gate_cols[:, t], ident_bf16[:])
 
-        idle_ps = idle.tile([P, PIECE], F32)
+        idle_ps = idle.tile([P, HALF], F32)
 
-        def idle_pass():
-            nc.tensor.matmul_mx(
-                out=idle_ps[:],
-                lhsT=w1_codes[:, 0, 0:P].bitcast(FP8X4),
-                lhsT_scale=w1_scales[:, 0, 0:P],
-                rhs=w1_codes[:, 0, :].bitcast(FP8X4),
-                rhs_scale=w1_scales[:, 0, :],
-                start=True,
-                stop=True,
-            )
+        def idle_passes(codes, scales):
+            for i in range(IDLE_PASSES):
+                nc.tensor.matmul_mx(
+                    out=idle_ps[:],
+                    lhsT=codes[:, 0:P].bitcast(FP8X4),
+                    lhsT_scale=scales[:, 0:P],
+                    rhs=codes.bitcast(FP8X4),
+                    rhs_scale=scales,
+                    start=True,
+                    stop=True,
+                )
 
-        for i in range(IDLE_PASSES):
-            idle_pass()
+        idle_passes(w1_codes[:, 0, 0:HALF], w1_scales[:, 0, 0:HALF])
 
         a_ps = [psum.tile([P, ROWS], F32, tag="bank", name="a_ps%d" % c) for c in range(CHUNKS_1)]
         regroup_w1(1)
@@ -182,9 +183,12 @@ def tile_node_interaction_s_kernel(
         def regroup_w2(copy, i, first, last):
             regroup(copy, w2_grouped[i][:], w2_raw[i][:], first, last)
 
-        def quantise_w2(i):
+        def quantise_w2(i, first, last):
             quantise(
-                nc, w2_codes[i][:], w2_scales[i][:], w2_grouped[i][:].rearrange("p w j -> p (w j)")
+                nc,
+                w2_codes[i][:, first:last],
+                w2_scales[i][:, first:last],
+                w2_grouped[i][:, first:last, :].rearrange("p w j -> p (w j)"),
             )
 
         regroup_w2(nc.vector.tensor_copy, 0, 0, VECTOR_W2[0])
@@ -198,14 +202,8 @@ def tile_node_interaction_s_kernel(
         nc.scalar.copy(out=bias_t[:], in_=bias_ps[:, 0:CHUNKS_2])
         regroup_w2(nc.vector.tensor_copy, 1, 0, VECTOR_W2[1])
         regroup_w2(nc.scalar.copy, 1, VECTOR_W2[1], PIECE)
-        nc.tensor.matmul(
-            out=idle_ps[:],
-            lhsT=ident_bf16[:],
-            rhs=w2_grouped[1][:, 0:P, :].rearrange("p w j -> p (w j)"),
-            start=True,
-            stop=True,
-        )
-        idle_pass()
+        quantise_w2(0, 0, HALF)
+        idle_passes(w2_codes[0][:, 0:HALF], w2_scales[0][:, 0:HALF])
         h_grouped = sbuf.tile([P, 2, E, PACK], BF16, align_bytes=64)
         gate_rows = gate_ps[:, :, 0:E].rearrange("p t e -> p e t")
         nc.vector.tensor_tensor(
@@ -214,11 +212,11 @@ def tile_node_interaction_s_kernel(
             in1=gate_rows.unsqueeze(1).to_broadcast([P, 2, E, PACK]),
             op=MULT,
         )
-        quantise_w2(0)
+        quantise_w2(0, HALF, PIECE)
         h_codes = sbuf.tile([P, ROWS], U32, align_bytes=64)
         h_scales = sbuf.tile([P, ROWS], U8, align_bytes=64)
         quantise(nc, h_codes[:], h_scales[:], h_grouped[:].rearrange("p half e t -> p (half e t)"))
-        quantise_w2(1)
+        quantise_w2(1, 0, PIECE)
 
         y_t = []
         for pair in range(PAIRS):

@@ -24,8 +24,8 @@ IDLE_PASSES = 4
 PIECES_2 = D // PIECE
 CHUNKS_PIECE = PIECE // P
 RUN = 8
-VECTOR_W1 = (320, 320)
-VECTOR_W2 = (256, 224)
+VECTOR_W1 = (352, 352)
+VECTOR_W2 = (288, 224)
 
 FLOPS = 2 * ROWS * D * H + 2 * ROWS * H * D
 

import concourse.mybir as mybir
from concourse.masks import make_identity

F32 = mybir.dt.float32
BF16 = mybir.dt.bfloat16
U32 = mybir.dt.uint32
U8 = mybir.dt.uint8
FP8X4 = mybir.dt.float8_e4m3fn_x4
SILU = mybir.ActivationFunctionType.Silu
MULT = mybir.AluOpType.mult

P = 128
PACK = 4
K_PASS = P * PACK
E, D, H = 64, 1024, 512
ROWS = 2 * E
PASSES_1 = D // K_PASS
CHUNKS_1 = H // P
CHUNKS_2 = D // P
PAIRS = CHUNKS_2 // 2
PIECE = 512
HALF = PIECE // 2
IDLE_PASSES = 4
PIECES_2 = D // PIECE
CHUNKS_PIECE = PIECE // P
RUN = 8
VECTOR_W1 = (352, 352)
VECTOR_W2 = (288, 224)

FLOPS = 2 * ROWS * D * H + 2 * ROWS * H * D


def regroup_permuted(copy, grouped, raw, first, last):
    m = slice(first // PACK, last // PACK)
    copy(
        out=grouped.rearrange("p (t m) j -> p m j t", t=PACK)[:, m],
        in_=raw.rearrange("p j (m t) -> p m j t", t=PACK)[:, m],
    )


def regroup(copy, grouped, raw, first, last):
    copy(
        out=grouped[:, first:last, :].rearrange("p (c i) j -> p c j i", i=RUN),
        in_=raw[:, :, first:last].rearrange("p j (c i) -> p c j i", i=RUN),
    )


def quantise(nc, codes, scales, grouped):
    nc.vector.quantize_mx(out=codes.bitcast(FP8X4), scales=scales, in_=grouped)


def tile_node_interaction_s_kernel(
    tc, node_embed, x_edge_c, ori, W1, b1, W2, b2, edge_num, out
):
    nc = tc.nc
    assert edge_num == E

    with tc.tile_pool(name="sbuf", bufs=1) as sbuf, tc.psum_pool(
        name="psum", bufs=7
    ) as psum, tc.psum_pool(name="idle", bufs=1) as idle, tc.manual_schedule():
        gate_sb = sbuf.tile([P, H], BF16)
        nc.vector.memset(gate_sb[E:P, :], 0.0)
        nc.scalar.dma_start(out=gate_sb[0:E, :], in_=x_edge_c)
        b1_t = sbuf.tile([P, CHUNKS_1], BF16)
        nc.scalar.dma_start(out=b1_t[:], in_=b1.rearrange("(p t) -> p t", t=PACK))
        bias_rows = sbuf.tile([P, P], BF16)
        nc.vector.memset(bias_rows[:], 0.0)
        nc.scalar.dma_start(out=bias_rows[0:CHUNKS_2, :], in_=b2.rearrange("(c p) -> c p", p=P))
        w1_raw = sbuf.tile([P, PASSES_1, PACK, H], BF16)
        w1_rows = W1.rearrange("(g p j) c -> g p j c", g=PASSES_1, j=PACK)
        nc.sync.dma_start(out=w1_raw[:, 0], in_=w1_rows[0])
        x_sb = sbuf.tile([P, 2, K_PASS], BF16)
        for half, x_half in enumerate((node_embed, ori)):
            nc.sync.dma_start(
                out=x_sb[:, half, :], in_=x_half.rearrange("e (g k) -> (e g) k", g=PASSES_1)
            )
        nc.sync.dma_start(out=w1_raw[:, 1], in_=w1_rows[1])
        w2_rows = W2.rearrange("(p j) n -> p j n", j=PACK)
        w2_raw = []
        for i in range(PIECES_2):
            raw = sbuf.tile([P, PACK, PIECE], BF16, name="w2_raw%d" % i)
            nc.sync.dma_start(out=raw[:], in_=w2_rows[:, :, i * PIECE : (i + 1) * PIECE])
            w2_raw.append(raw)

        ident_f32 = sbuf.tile([P, P], F32)
        make_identity(nc, ident_f32[:])
        ident_bf16 = sbuf.tile([P, P], BF16)
        make_identity(nc, ident_bf16[:])
        warm = sbuf.tile([P, 1], F32)
        nc.vector.memset(warm[:], 0.0)
        nc.scalar.activation(out=warm[:], in_=warm[:], func=SILU)

        w1_grouped = sbuf.tile([P, PASSES_1, H, PACK], BF16, align_bytes=64)
        w1_codes = sbuf.tile([P, PASSES_1, H], U32, align_bytes=64)
        w1_scales = sbuf.tile([P, PASSES_1, H], U8, align_bytes=64)

        def quantise_w1(g):
            quantise(
                nc, w1_codes[:, g], w1_scales[:, g], w1_grouped[:, g].rearrange("p w j -> p (w j)")
            )

        def regroup_w1(g):
            cut = VECTOR_W1[g]
            regroup_permuted(nc.vector.tensor_copy, w1_grouped[:, g], w1_raw[:, g], 0, cut)
            regroup_permuted(nc.scalar.copy, w1_grouped[:, g], w1_raw[:, g], cut, H)

        regroup_w1(0)
        quantise_w1(0)

        x_grouped = sbuf.tile([P, PASSES_1 * ROWS * PACK], BF16, align_bytes=64)
        x_grouped_words = x_grouped[:].bitcast(F32).rearrange(
            "p (g half e u) -> p half g e u", g=PASSES_1, half=2, u=2
        )
        x_words = x_sb[:].bitcast(F32).rearrange("q half (p u) -> q half u p", u=2)
        for half in range(2):
            xt_ps = psum.tile([P, 2, E, PASSES_1], F32, tag="bank")
            for u in range(2):
                nc.tensor.transpose(
                    xt_ps[:, u].rearrange("p e g -> p (e g)"), x_words[:, half, u, :], ident_f32[:]
                )
            nc.scalar.copy(
                out=x_grouped_words[:, half], in_=xt_ps[:].rearrange("p u e g -> p g e u")
            )
        x_codes = sbuf.tile([P, PASSES_1, ROWS], U32, align_bytes=64)
        x_scales = sbuf.tile([P, PASSES_1, ROWS], U8, align_bytes=64)

        gate_ps = psum.tile([P, PACK, P], BF16, tag="bank")
        gate_cols = gate_sb[:].rearrange("e (m t) -> e t m", t=PACK)
        for t in range(PACK):
            nc.tensor.transpose(gate_ps[:, t], gate_cols[:, t], ident_bf16[:])

        idle_ps = idle.tile([P, HALF], F32)

        def idle_passes(codes, scales):
            for i in range(IDLE_PASSES):
                nc.tensor.matmul_mx(
                    out=idle_ps[:],
                    lhsT=codes[:, 0:P].bitcast(FP8X4),
                    lhsT_scale=scales[:, 0:P],
                    rhs=codes.bitcast(FP8X4),
                    rhs_scale=scales,
                    start=True,
                    stop=True,
                )

        idle_passes(w1_codes[:, 0, 0:HALF], w1_scales[:, 0, 0:HALF])

        a_ps = [psum.tile([P, ROWS], F32, tag="bank", name="a_ps%d" % c) for c in range(CHUNKS_1)]
        regroup_w1(1)
        quantise(
            nc,
            x_codes[:].rearrange("p g r -> p (g r)"),
            x_scales[:].rearrange("p g r -> p (g r)"),
            x_grouped[:],
        )
        quantise_w1(1)
        for g in range(PASSES_1):
            for c in range(CHUNKS_1):
                nc.tensor.matmul_mx(
                    out=a_ps[c][:],
                    lhsT=w1_codes[:, g, c * P : (c + 1) * P].bitcast(FP8X4),
                    lhsT_scale=w1_scales[:, g, c * P : (c + 1) * P],
                    rhs=x_codes[:, g, :].bitcast(FP8X4),
                    rhs_scale=x_scales[:, g, :],
                    start=(g == 0),
                    stop=(g == PASSES_1 - 1),
                )

        bias_ps = psum.tile([P, P], BF16, tag="bank")
        nc.tensor.transpose(bias_ps[:], bias_rows[:], ident_bf16[:])

        w2_grouped = []
        w2_codes = []
        w2_scales = []
        for i in range(PIECES_2):
            grouped = sbuf.tile([P, PIECE, PACK], BF16, align_bytes=64, name="w2_grouped%d" % i)
            codes = sbuf.tile([P, PIECE], U32, align_bytes=64, name="w2_codes%d" % i)
            scales = sbuf.tile([P, PIECE], U8, align_bytes=64, name="w2_scales%d" % i)
            w2_grouped.append(grouped)
            w2_codes.append(codes)
            w2_scales.append(scales)

        def regroup_w2(copy, i, first, last):
            regroup(copy, w2_grouped[i][:], w2_raw[i][:], first, last)

        def quantise_w2(i, first, last):
            quantise(
                nc,
                w2_codes[i][:, first:last],
                w2_scales[i][:, first:last],
                w2_grouped[i][:, first:last, :].rearrange("p w j -> p (w j)"),
            )

        regroup_w2(nc.vector.tensor_copy, 0, 0, VECTOR_W2[0])
        regroup_w2(nc.scalar.copy, 0, VECTOR_W2[0], PIECE)
        a_t = sbuf.tile([P, CHUNKS_1, ROWS], F32)
        for c in range(CHUNKS_1):
            nc.scalar.activation(
                out=a_t[:, c, :], in_=a_ps[c][:], func=SILU, bias=b1_t[:, c : c + 1], scale=1.0
            )
        bias_t = sbuf.tile([P, CHUNKS_2], F32)
        nc.scalar.copy(out=bias_t[:], in_=bias_ps[:, 0:CHUNKS_2])
        regroup_w2(nc.vector.tensor_copy, 1, 0, VECTOR_W2[1])
        regroup_w2(nc.scalar.copy, 1, VECTOR_W2[1], PIECE)
        quantise_w2(0, 0, HALF)
        idle_passes(w2_codes[0][:, 0:HALF], w2_scales[0][:, 0:HALF])
        h_grouped = sbuf.tile([P, 2, E, PACK], BF16, align_bytes=64)
        gate_rows = gate_ps[:, :, 0:E].rearrange("p t e -> p e t")
        nc.vector.tensor_tensor(
            out=h_grouped[:],
            in0=a_t[:].rearrange("p t (half e) -> p half e t", half=2),
            in1=gate_rows.unsqueeze(1).to_broadcast([P, 2, E, PACK]),
            op=MULT,
        )
        quantise_w2(0, HALF, PIECE)
        h_codes = sbuf.tile([P, ROWS], U32, align_bytes=64)
        h_scales = sbuf.tile([P, ROWS], U8, align_bytes=64)
        quantise(nc, h_codes[:], h_scales[:], h_grouped[:].rearrange("p half e t -> p (half e t)"))
        quantise_w2(1, 0, PIECE)

        y_t = []
        for pair in range(PAIRS):
            y_pair = sbuf.tile([P, 2, 2, E], F32, name="y_t%d" % pair)
            y_t.append(y_pair)

        def layer_2_chunk(c):
            piece, place = divmod(c, CHUNKS_PIECE)
            cols = slice(place * P, (place + 1) * P)
            y_ps = psum.tile([P, ROWS], F32, tag="bank")
            nc.tensor.matmul_mx(
                out=y_ps[:],
                lhsT=w2_codes[piece][:, cols].bitcast(FP8X4),
                lhsT_scale=w2_scales[piece][:, cols],
                rhs=h_codes[:].bitcast(FP8X4),
                rhs_scale=h_scales[:],
                start=True,
                stop=True,
            )
            nc.scalar.activation(
                out=y_t[c // 2][:, :, c % 2, :],
                in_=y_ps[:].rearrange("p (half e) -> p half e", half=2),
                func=SILU,
                bias=bias_t[:, c : c + 1],
                scale=1.0,
            )

        out_sb = sbuf.tile([P, PAIRS, P], F32)
        out_rows = out.rearrange("e (pair i) d -> i e pair d", i=2)

        def close_pair(pair):
            out_ps = psum.tile([P, P], F32, tag="bank")
            for half in range(2):
                nc.tensor.matmul(
                    out=out_ps[:],
                    lhsT=y_t[pair][:, half].rearrange("p i e -> p (i e)"),
                    rhs=ident_f32[:],
                    start=(half == 0),
                    stop=(half == 1),
                    is_transpose=True,
                )
            nc.vector.tensor_copy(out=out_sb[:, pair, :], in_=out_ps[:])
            if pair % 2 == 1:
                done = slice(pair - 1, pair + 1)
                for i in range(2):
                    nc.sync.dma_start(
                        out=out_rows[i][:, done, :], in_=out_sb[i * E : (i + 1) * E, done, :]
                    )

        for c in range(CHUNKS_2):
            layer_2_chunk(c)
        for pair in range(PAIRS):
            close_pair(pair)
